import numpy as np
import ml_dtypes

BF16 = ml_dtypes.bfloat16


def bf(x):
    return np.asarray(x, np.float32).astype(BF16)


def f32(x):
    return np.asarray(x, np.float32)


def f64(x):
    return np.asarray(x).astype(np.float64)


def striped(idx):
    return np.tile(idx.reshape(-1, 16).T, (8, 1))


H, T, C, S, N = 128, 4, 512, 1024, 512


def sigmoid(v):
    return 1.0 / (1.0 + np.exp(-v))


def setup_inputs():
    return {"base": f32(np.random.standard_normal((C, S))), "mem_old": f32(np.random.standard_normal((C, N))), "emb": f32(np.random.standard_normal((H, N))), "fw_emb": f32(np.random.standard_normal((H, 1)) / np.sqrt(H)), "fw_mem": f32(np.random.standard_normal((H, 1)) / np.sqrt(H)), "offs": striped(np.random.permutation(S)[:N])}


def reference(base, mem_old, emb, fw_emb, fw_mem, offs):
    idx = offs[:16].T.reshape(-1)
    old = f64(mem_old).reshape(T, H, N)
    e = f64(emb)
    logit = (f64(fw_emb) * e).sum(axis=0)[None, :] + (f64(fw_mem)[None, :, :] * old).sum(axis=1)
    gate = sigmoid(logit)[:, None, :]
    new = old * (1.0 - gate) + e[None, :, :] * gate
    res = f64(base).copy()
    res[:, idx] = new.reshape(C, N)
    return res

@@ -1,0 +1,58 @@
+import concourse.mybir as mybir
+
+H, T, S, N = 128, 4, 1024, 512
+F32, BF16, U16 = mybir.dt.float32, mybir.dt.bfloat16, mybir.dt.uint16
+ADD, MULT = mybir.AluOpType.add, mybir.AluOpType.mult
+SIGMOID = mybir.ActivationFunctionType.Sigmoid
+
+FLOPS = 2 * H * N * (T + 1)
+
+
+def tile_memory_s_kernel(tc, base, mem_old, emb, fw_emb, fw_mem, offs, out):
+    nc = tc.nc
+    with (
+        tc.tile_pool(name="held", bufs=1) as held,
+        tc.tile_pool(name="slots", bufs=T) as slots,
+        tc.psum_pool(name="psum", bufs=T) as psum,
+    ):
+        offsets = held.tile([H, N // 16], U16, name="offsets")
+        nc.sync.dma_start(offsets[:], offs)
+        column_emb = held.tile([H, 1], F32, name="column_emb")
+        nc.scalar.dma_start(column_emb[:], fw_emb)
+        column_mem = held.tile([H, 1], F32, name="column_mem")
+        nc.scalar.dma_start(column_mem[:], fw_mem)
+        emb_f32 = held.tile([H, N], F32, name="emb_f32")
+        nc.scalar.dma_start(emb_f32[:], emb)
+        olds, windows = [], []
+        for t in range(T):
+            old = slots.tile([H, N], F32, name="old")
+            nc.sync.dma_start(old[:], mem_old[t * H : (t + 1) * H, :])
+            olds.append(old)
+            window = slots.tile([H, S], F32, name="window")
+            nc.sync.dma_start(window[:], base[t * H : (t + 1) * H, :])
+            windows.append(window)
+
+        spread_emb = held.tile([H, H], BF16, name="spread_emb")
+        nc.vector.tensor_copy(spread_emb[:], column_emb[:].to_broadcast([H, H]))
+        spread_mem = held.tile([H, H], BF16, name="spread_mem")
+        nc.vector.tensor_copy(spread_mem[:], column_mem[:].to_broadcast([H, H]))
+        emb_bf16 = held.tile([H, N], BF16, name="emb_bf16")
+        nc.scalar.copy(emb_bf16[:], emb_f32[:])
+
+        for t in range(T):
+            old, window = olds[t], windows[t]
+            old_bf16 = slots.tile([H, N], BF16, name="old_bf16")
+            nc.scalar.copy(old_bf16[:], old[:])
+            logit = psum.tile([H, N], F32, name="logit")
+            nc.tensor.matmul(logit[:], spread_emb[:], emb_bf16[:], start=True, stop=False)
+            nc.tensor.matmul(logit[:], spread_mem[:], old_bf16[:], start=False, stop=True)
+            gate = slots.tile([H, N], F32, name="gate")
+            nc.scalar.activation(gate[:], logit[:], SIGMOID)
+            keep = slots.tile([H, N], F32, name="keep")
+            nc.scalar.activation(keep[:], logit[:], SIGMOID, scale=-1.0)
+            kept = slots.tile([H, N], F32, name="kept")
+            nc.vector.tensor_tensor(kept[:], old[:], keep[:], MULT)
+            written = slots.tile([H, N], F32, name="written")
+            nc.vector.tensor_tensor(written[:], emb_f32[:], gate[:], MULT)
+            nc.vector.tensor_tensor(window[:].indirect(offsets[:]), kept[:], written[:], ADD)
+            nc.sync.dma_start(out[t * H : (t + 1) * H, :], window[:])

@@ -51,8 +51,8 @@ def tile_memory_s_kernel(tc, base, mem_old, emb, fw_emb, fw_mem, offs, out):
             keep = slots.tile([H, N], F32, name="keep")
             nc.scalar.activation(keep[:], logit[:], SIGMOID, scale=-1.0)
             kept = slots.tile([H, N], F32, name="kept")
-            nc.vector.tensor_tensor(kept[:], old[:], keep[:], MULT)
+            nc.gpsimd.tensor_tensor(kept[:], old[:], keep[:], MULT)
             written = slots.tile([H, N], F32, name="written")
-            nc.vector.tensor_tensor(written[:], emb_f32[:], gate[:], MULT)
+            nc.gpsimd.tensor_tensor(written[:], emb_f32[:], gate[:], MULT)
             nc.vector.tensor_tensor(window[:].indirect(offsets[:]), kept[:], written[:], ADD)
             nc.sync.dma_start(out[t * H : (t + 1) * H, :], window[:])

@@ -22,7 +22,7 @@ def tile_memory_s_kernel(tc, base, mem_old, emb, fw_emb, fw_mem, offs, out):
         column_mem = held.tile([H, 1], F32, name="column_mem")
         nc.scalar.dma_start(column_mem[:], fw_mem)
         emb_f32 = held.tile([H, N], F32, name="emb_f32")
-        nc.scalar.dma_start(emb_f32[:], emb)
+        nc.sync.dma_start(emb_f32[:], emb)
         olds, windows = [], []
         for t in range(T):
             old = slots.tile([H, N], F32, name="old")
@@ -37,22 +37,25 @@ def tile_memory_s_kernel(tc, base, mem_old, emb, fw_emb, fw_mem, offs, out):
         spread_mem = held.tile([H, H], BF16, name="spread_mem")
         nc.vector.tensor_copy(spread_mem[:], column_mem[:].to_broadcast([H, H]))
         emb_bf16 = held.tile([H, N], BF16, name="emb_bf16")
-        nc.scalar.copy(emb_bf16[:], emb_f32[:])
+        nc.vector.tensor_copy(emb_bf16[:], emb_f32[:])
 
         for t in range(T):
             old, window = olds[t], windows[t]
             old_bf16 = slots.tile([H, N], BF16, name="old_bf16")
-            nc.scalar.copy(old_bf16[:], old[:])
+            if t == 0:
+                nc.vector.tensor_copy(old_bf16[:], old[:])
+            else:
+                nc.scalar.copy(old_bf16[:], old[:])
             logit = psum.tile([H, N], F32, name="logit")
             nc.tensor.matmul(logit[:], spread_emb[:], emb_bf16[:], start=True, stop=False)
             nc.tensor.matmul(logit[:], spread_mem[:], old_bf16[:], start=False, stop=True)
             gate = slots.tile([H, N], F32, name="gate")
             nc.scalar.activation(gate[:], logit[:], SIGMOID)
+            written = slots.tile([H, N], F32, name="written")
+            nc.vector.tensor_tensor(written[:], emb_f32[:], gate[:], MULT)
             keep = slots.tile([H, N], F32, name="keep")
             nc.scalar.activation(keep[:], logit[:], SIGMOID, scale=-1.0)
             kept = slots.tile([H, N], F32, name="kept")
-            nc.gpsimd.tensor_tensor(kept[:], old[:], keep[:], MULT)
-            written = slots.tile([H, N], F32, name="written")
-            nc.gpsimd.tensor_tensor(written[:], emb_f32[:], gate[:], MULT)
+            nc.vector.tensor_tensor(kept[:], old[:], keep[:], MULT)
             nc.vector.tensor_tensor(window[:].indirect(offsets[:]), kept[:], written[:], ADD)
             nc.sync.dma_start(out[t * H : (t + 1) * H, :], window[:])

@@ -32,6 +32,11 @@ def tile_memory_s_kernel(tc, base, mem_old, emb, fw_emb, fw_mem, offs, out):
             nc.sync.dma_start(window[:], base[t * H : (t + 1) * H, :])
             windows.append(window)
 
+        zeros = held.tile([H, 1], F32, name="zeros")
+        nc.vector.memset(zeros[:], 0.0)
+        halves = held.tile([H, 1], F32, name="halves")
+        nc.scalar.activation(halves[:], zeros[:], SIGMOID)
+
         spread_emb = held.tile([H, H], BF16, name="spread_emb")
         nc.vector.tensor_copy(spread_emb[:], column_emb[:].to_broadcast([H, H]))
         spread_mem = held.tile([H, H], BF16, name="spread_mem")

@@ -7,60 +7,65 @@ SIGMOID = mybir.ActivationFunctionType.Sigmoid
 
 FLOPS = 2 * H * N * (T + 1)
 
+FIRST_PIECES = 2
+
+
+def column_pieces(pieces):
+    width = N // pieces
+    return [(piece * width, (piece + 1) * width) for piece in range(pieces)]
+
 
 def tile_memory_s_kernel(tc, base, mem_old, emb, fw_emb, fw_mem, offs, out):
     nc = tc.nc
     with (
         tc.tile_pool(name="held", bufs=1) as held,
         tc.tile_pool(name="slots", bufs=T) as slots,
-        tc.psum_pool(name="psum", bufs=T) as psum,
+        tc.psum_pool(name="psum", bufs=FIRST_PIECES + T - 1) as psum,
     ):
-        offsets = held.tile([H, N // 16], U16, name="offsets")
-        nc.sync.dma_start(offsets[:], offs)
         column_emb = held.tile([H, 1], F32, name="column_emb")
         nc.scalar.dma_start(column_emb[:], fw_emb)
         column_mem = held.tile([H, 1], F32, name="column_mem")
         nc.scalar.dma_start(column_mem[:], fw_mem)
         emb_f32 = held.tile([H, N], F32, name="emb_f32")
-        nc.sync.dma_start(emb_f32[:], emb)
-        olds, windows = [], []
-        for t in range(T):
-            old = slots.tile([H, N], F32, name="old")
-            nc.sync.dma_start(old[:], mem_old[t * H : (t + 1) * H, :])
-            olds.append(old)
-            window = slots.tile([H, S], F32, name="window")
-            nc.sync.dma_start(window[:], base[t * H : (t + 1) * H, :])
-            windows.append(window)
-
-        zeros = held.tile([H, 1], F32, name="zeros")
-        nc.vector.memset(zeros[:], 0.0)
-        halves = held.tile([H, 1], F32, name="halves")
-        nc.scalar.activation(halves[:], zeros[:], SIGMOID)
+        olds = [slots.tile([H, N], F32, name="old") for t in range(T)]
+        windows = [slots.tile([H, S], F32, name="window") for t in range(T)]
+        for first, end in column_pieces(FIRST_PIECES):
+            nc.sync.dma_start(emb_f32[:, first:end], emb[:, first:end])
+            nc.sync.dma_start(olds[0][:, first:end], mem_old[0:H, first:end])
+        offsets = held.tile([H, N // 16], U16, name="offsets")
+        nc.sync.dma_start(offsets[:], offs)
+        nc.sync.dma_start(windows[0][:], base[0:H, :])
+        for t in range(1, T):
+            nc.sync.dma_start(olds[t][:], mem_old[t * H : (t + 1) * H, :])
+            nc.sync.dma_start(windows[t][:], base[t * H : (t + 1) * H, :])
 
         spread_emb = held.tile([H, H], BF16, name="spread_emb")
         nc.vector.tensor_copy(spread_emb[:], column_emb[:].to_broadcast([H, H]))
         spread_mem = held.tile([H, H], BF16, name="spread_mem")
         nc.vector.tensor_copy(spread_mem[:], column_mem[:].to_broadcast([H, H]))
         emb_bf16 = held.tile([H, N], BF16, name="emb_bf16")
-        nc.vector.tensor_copy(emb_bf16[:], emb_f32[:])
+        for first, end in column_pieces(FIRST_PIECES):
+            nc.vector.tensor_copy(emb_bf16[:, first:end], emb_f32[:, first:end])
 
         for t in range(T):
             old, window = olds[t], windows[t]
             old_bf16 = slots.tile([H, N], BF16, name="old_bf16")
-            if t == 0:
-                nc.vector.tensor_copy(old_bf16[:], old[:])
-            else:
-                nc.scalar.copy(old_bf16[:], old[:])
-            logit = psum.tile([H, N], F32, name="logit")
-            nc.tensor.matmul(logit[:], spread_emb[:], emb_bf16[:], start=True, stop=False)
-            nc.tensor.matmul(logit[:], spread_mem[:], old_bf16[:], start=False, stop=True)
             gate = slots.tile([H, N], F32, name="gate")
-            nc.scalar.activation(gate[:], logit[:], SIGMOID)
-            written = slots.tile([H, N], F32, name="written")
-            nc.vector.tensor_tensor(written[:], emb_f32[:], gate[:], MULT)
             keep = slots.tile([H, N], F32, name="keep")
-            nc.scalar.activation(keep[:], logit[:], SIGMOID, scale=-1.0)
+            written = slots.tile([H, N], F32, name="written")
             kept = slots.tile([H, N], F32, name="kept")
-            nc.vector.tensor_tensor(kept[:], old[:], keep[:], MULT)
+            for first, end in column_pieces(FIRST_PIECES if t == 0 else 1):
+                if t == 0:
+                    nc.vector.tensor_copy(old_bf16[:, first:end], old[:, first:end])
+                else:
+                    nc.scalar.copy(old_bf16[:, first:end], old[:, first:end])
+                bank = psum.tile([H, N], F32, name="bank")
+                logit = bank[:, 0 : end - first]
+                nc.tensor.matmul(logit, spread_emb[:], emb_bf16[:, first:end], start=True, stop=False)
+                nc.tensor.matmul(logit, spread_mem[:], old_bf16[:, first:end], start=False, stop=True)
+                nc.scalar.activation(gate[:, first:end], logit, SIGMOID)
+                nc.vector.tensor_tensor(written[:, first:end], emb_f32[:, first:end], gate[:, first:end], MULT)
+                nc.scalar.activation(keep[:, first:end], logit, SIGMOID, scale=-1.0)
+                nc.vector.tensor_tensor(kept[:, first:end], old[:, first:end], keep[:, first:end], MULT)
             nc.vector.tensor_tensor(window[:].indirect(offsets[:]), kept[:], written[:], ADD)
             nc.sync.dma_start(out[t * H : (t + 1) * H, :], window[:])

@@ -1,9 +1,11 @@
 import concourse.mybir as mybir
+from concourse.masks import make_identity
 
 H, T, S, N = 128, 4, 1024, 512
+B = N // H
 F32, BF16, U16 = mybir.dt.float32, mybir.dt.bfloat16, mybir.dt.uint16
 ADD, MULT = mybir.AluOpType.add, mybir.AluOpType.mult
-SIGMOID = mybir.ActivationFunctionType.Sigmoid
+SIGMOID, COPY = mybir.ActivationFunctionType.Sigmoid, mybir.ActivationFunctionType.Copy
 
 FLOPS = 2 * H * N * (T + 1)
 
@@ -17,10 +19,13 @@ def column_pieces(pieces):
 
 def tile_memory_s_kernel(tc, base, mem_old, emb, fw_emb, fw_mem, offs, out):
     nc = tc.nc
+    squares = column_pieces(B)
     with (
         tc.tile_pool(name="held", bufs=1) as held,
         tc.tile_pool(name="slots", bufs=T) as slots,
-        tc.psum_pool(name="psum", bufs=FIRST_PIECES + T - 1) as psum,
+        tc.psum_pool(name="psum_held", bufs=1) as psum_held,
+        tc.psum_pool(name="psum_turned", bufs=2) as psum_turned,
+        tc.psum_pool(name="psum_banks", bufs=4) as psum_banks,
     ):
         column_emb = held.tile([H, 1], F32, name="column_emb")
         nc.scalar.dma_start(column_emb[:], fw_emb)
@@ -32,12 +37,16 @@ def tile_memory_s_kernel(tc, base, mem_old, emb, fw_emb, fw_mem, offs, out):
         for first, end in column_pieces(FIRST_PIECES):
             nc.sync.dma_start(emb_f32[:, first:end], emb[:, first:end])
             nc.sync.dma_start(olds[0][:, first:end], mem_old[0:H, first:end])
+        nc.sync.dma_start(olds[1][:], mem_old[H : 2 * H, :])
         offsets = held.tile([H, N // 16], U16, name="offsets")
         nc.sync.dma_start(offsets[:], offs)
-        nc.sync.dma_start(windows[0][:], base[0:H, :])
-        for t in range(1, T):
-            nc.sync.dma_start(olds[t][:], mem_old[t * H : (t + 1) * H, :])
+        for t in range(T):
             nc.sync.dma_start(windows[t][:], base[t * H : (t + 1) * H, :])
+            if t + 2 < T:
+                nc.sync.dma_start(olds[t + 2][:], mem_old[(t + 2) * H : (t + 3) * H, :])
+
+        identity = held.tile([H, H], F32, name="identity")
+        make_identity(nc, identity[:])
 
         spread_emb = held.tile([H, H], BF16, name="spread_emb")
         nc.vector.tensor_copy(spread_emb[:], column_emb[:].to_broadcast([H, H]))
@@ -47,25 +56,70 @@ def tile_memory_s_kernel(tc, base, mem_old, emb, fw_emb, fw_mem, offs, out):
         for first, end in column_pieces(FIRST_PIECES):
             nc.vector.tensor_copy(emb_bf16[:, first:end], emb_f32[:, first:end])
 
-        for t in range(T):
-            old, window = olds[t], windows[t]
+        kepts = [slots.tile([H, N], F32, name="kept") for t in range(T)]
+        writtens = [slots.tile([H, N], F32, name="written") for t in range(T)]
+
+        def place(t):
+            nc.vector.tensor_tensor(windows[t][:].indirect(offsets[:]), kepts[t][:], writtens[t][:], ADD)
+            nc.sync.dma_start(out[t * H : (t + 1) * H, :], windows[t][:])
+
+        old0_bf16 = held.tile([H, N], BF16, name="old0_bf16")
+        gate = held.tile([H, N], F32, name="gate")
+        keep = held.tile([H, N], F32, name="keep")
+        for first, end in column_pieces(FIRST_PIECES):
+            nc.vector.tensor_copy(old0_bf16[:, first:end], olds[0][:, first:end])
+            bank = psum_banks.tile([H, N], F32, name="bank")
+            logit = bank[:, 0 : end - first]
+            nc.tensor.matmul(logit, spread_emb[:], emb_bf16[:, first:end], start=True, stop=False)
+            nc.tensor.matmul(logit, spread_mem[:], old0_bf16[:, first:end], start=False, stop=True)
+            nc.scalar.activation(gate[:, first:end], logit, SIGMOID)
+            nc.vector.tensor_tensor(writtens[0][:, first:end], emb_f32[:, first:end], gate[:, first:end], MULT)
+            nc.scalar.activation(keep[:, first:end], logit, SIGMOID, scale=-1.0)
+            nc.vector.tensor_tensor(kepts[0][:, first:end], olds[0][:, first:end], keep[:, first:end], MULT)
+
+        emb_turned = psum_held.tile([H, N], F32, name="emb_turned")
+        for first, end in squares:
+            nc.tensor.transpose(emb_turned[:, first:end], emb_f32[:, first:end], identity[:])
+
+        old_turneds, gate_columns, keep_columns = {}, {}, {}
+
+        def front(t):
             old_bf16 = slots.tile([H, N], BF16, name="old_bf16")
-            gate = slots.tile([H, N], F32, name="gate")
-            keep = slots.tile([H, N], F32, name="keep")
-            written = slots.tile([H, N], F32, name="written")
-            kept = slots.tile([H, N], F32, name="kept")
-            for first, end in column_pieces(FIRST_PIECES if t == 0 else 1):
-                if t == 0:
-                    nc.vector.tensor_copy(old_bf16[:, first:end], old[:, first:end])
-                else:
-                    nc.scalar.copy(old_bf16[:, first:end], old[:, first:end])
-                bank = psum.tile([H, N], F32, name="bank")
-                logit = bank[:, 0 : end - first]
-                nc.tensor.matmul(logit, spread_emb[:], emb_bf16[:, first:end], start=True, stop=False)
-                nc.tensor.matmul(logit, spread_mem[:], old_bf16[:, first:end], start=False, stop=True)
-                nc.scalar.activation(gate[:, first:end], logit, SIGMOID)
-                nc.vector.tensor_tensor(written[:, first:end], emb_f32[:, first:end], gate[:, first:end], MULT)
-                nc.scalar.activation(keep[:, first:end], logit, SIGMOID, scale=-1.0)
-                nc.vector.tensor_tensor(kept[:, first:end], old[:, first:end], keep[:, first:end], MULT)
-            nc.vector.tensor_tensor(window[:].indirect(offsets[:]), kept[:], written[:], ADD)
-            nc.sync.dma_start(out[t * H : (t + 1) * H, :], window[:])
+            nc.scalar.copy(old_bf16[:], olds[t][:])
+            old_turneds[t] = psum_turned.tile([H, N], F32, name="old_turned")
+            for first, end in squares:
+                nc.tensor.transpose(old_turneds[t][:, first:end], olds[t][:, first:end], identity[:])
+            logit_columns = psum_held.tile([H, B], F32, name="logit_columns")
+            for b, (first, end) in enumerate(squares):
+                nc.tensor.matmul(logit_columns[:, b : b + 1], emb_bf16[:, first:end], spread_emb[:, 0:1], start=True, stop=False)
+                nc.tensor.matmul(logit_columns[:, b : b + 1], old_bf16[:, first:end], spread_mem[:, 0:1], start=False, stop=True)
+            gate_columns[t] = slots.tile([H, B], F32, name="gate_column")
+            nc.scalar.activation(gate_columns[t][:], logit_columns[:], SIGMOID)
+            keep_columns[t] = slots.tile([H, B], F32, name="keep_column")
+            nc.scalar.activation(keep_columns[t][:], logit_columns[:], SIGMOID, scale=-1.0)
+
+        kept_turneds, written_turneds = {}, {}
+
+        def middle(t):
+            kept_turneds[t] = slots.tile([H, N], F32, name="kept_turned")
+            for b, (first, end) in enumerate(squares):
+                nc.scalar.activation(kept_turneds[t][:, first:end], old_turneds[t][:, first:end], COPY, scale=keep_columns[t][:, b : b + 1])
+            written_turneds[t] = slots.tile([H, N], F32, name="written_turned")
+            for b, (first, end) in enumerate(squares):
+                nc.scalar.activation(written_turneds[t][:, first:end], emb_turned[:, first:end], COPY, scale=gate_columns[t][:, b : b + 1])
+
+        def back(t):
+            for turned, product in ((kept_turneds[t], kepts[t]), (written_turneds[t], writtens[t])):
+                bank = psum_banks.tile([H, N], F32, name="bank")
+                for first, end in squares:
+                    nc.tensor.transpose(bank[:, first:end], turned[:, first:end], identity[:])
+                nc.scalar.copy(product[:], bank[:])
+
+        front(1)
+        place(0)
+        for t in range(1, T):
+            middle(t)
+            if t + 1 < T:
+                front(t + 1)
+            back(t)
+            place(t)

@@ -11,6 +11,8 @@ FLOPS = 2 * H * N * (T + 1)
 
 FIRST_PIECES = 2
 
+VECTOR_BLOCKS = 2
+
 
 def column_pieces(pieces):
     width = N // pieces
@@ -34,19 +36,19 @@ def tile_memory_s_kernel(tc, base, mem_old, emb, fw_emb, fw_mem, offs, out):
         emb_f32 = held.tile([H, N], F32, name="emb_f32")
         olds = [slots.tile([H, N], F32, name="old") for t in range(T)]
         windows = [slots.tile([H, S], F32, name="window") for t in range(T)]
+        nc.gpsimd.dma_start(windows[0][:], base[0:H, :])
+        identity = held.tile([H, H], F32, name="identity")
+        make_identity(nc, identity[:])
+        for t in range(1, T):
+            nc.gpsimd.dma_start(windows[t][:], base[t * H : (t + 1) * H, :])
         for first, end in column_pieces(FIRST_PIECES):
             nc.sync.dma_start(emb_f32[:, first:end], emb[:, first:end])
             nc.sync.dma_start(olds[0][:, first:end], mem_old[0:H, first:end])
         nc.sync.dma_start(olds[1][:], mem_old[H : 2 * H, :])
         offsets = held.tile([H, N // 16], U16, name="offsets")
         nc.sync.dma_start(offsets[:], offs)
-        for t in range(T):
-            nc.sync.dma_start(windows[t][:], base[t * H : (t + 1) * H, :])
-            if t + 2 < T:
-                nc.sync.dma_start(olds[t + 2][:], mem_old[(t + 2) * H : (t + 3) * H, :])
-
-        identity = held.tile([H, H], F32, name="identity")
-        make_identity(nc, identity[:])
+        for t in range(2, T):
+            nc.sync.dma_start(olds[t][:], mem_old[t * H : (t + 1) * H, :])
 
         spread_emb = held.tile([H, H], BF16, name="spread_emb")
         nc.vector.tensor_copy(spread_emb[:], column_emb[:].to_broadcast([H, H]))
@@ -63,19 +65,29 @@ def tile_memory_s_kernel(tc, base, mem_old, emb, fw_emb, fw_mem, offs, out):
             nc.vector.tensor_tensor(windows[t][:].indirect(offsets[:]), kepts[t][:], writtens[t][:], ADD)
             nc.sync.dma_start(out[t * H : (t + 1) * H, :], windows[t][:])
 
-        old0_bf16 = held.tile([H, N], BF16, name="old0_bf16")
-        gate = held.tile([H, N], F32, name="gate")
-        keep = held.tile([H, N], F32, name="keep")
-        for first, end in column_pieces(FIRST_PIECES):
-            nc.vector.tensor_copy(old0_bf16[:, first:end], olds[0][:, first:end])
-            bank = psum_banks.tile([H, N], F32, name="bank")
-            logit = bank[:, 0 : end - first]
-            nc.tensor.matmul(logit, spread_emb[:], emb_bf16[:, first:end], start=True, stop=False)
-            nc.tensor.matmul(logit, spread_mem[:], old0_bf16[:, first:end], start=False, stop=True)
-            nc.scalar.activation(gate[:, first:end], logit, SIGMOID)
-            nc.vector.tensor_tensor(writtens[0][:, first:end], emb_f32[:, first:end], gate[:, first:end], MULT)
-            nc.scalar.activation(keep[:, first:end], logit, SIGMOID, scale=-1.0)
-            nc.vector.tensor_tensor(kepts[0][:, first:end], olds[0][:, first:end], keep[:, first:end], MULT)
+        old_bf16s, gates, keeps = {}, {}, {}
+
+        def gate_rows(t, pieces):
+            old_bf16s[t] = slots.tile([H, N], BF16, name="old_bf16")
+            gates[t] = slots.tile([H, N], F32, name="gate")
+            keeps[t] = slots.tile([H, N], F32, name="keep")
+            for first, end in column_pieces(pieces):
+                nc.vector.tensor_copy(old_bf16s[t][:, first:end], olds[t][:, first:end])
+                bank = psum_banks.tile([H, N], F32, name="bank")
+                logit = bank[:, 0 : end - first]
+                nc.tensor.matmul(logit, spread_emb[:], emb_bf16[:, first:end], start=True, stop=False)
+                nc.tensor.matmul(logit, spread_mem[:], old_bf16s[t][:, first:end], start=False, stop=True)
+                nc.scalar.activation(gates[t][:, first:end], logit, SIGMOID)
+                nc.scalar.activation(keeps[t][:, first:end], logit, SIGMOID, scale=-1.0)
+
+        def products_by_vector(t, pieces):
+            for first, end in column_pieces(pieces):
+                nc.vector.tensor_tensor(writtens[t][:, first:end], emb_f32[:, first:end], gates[t][:, first:end], MULT)
+                nc.vector.tensor_tensor(kepts[t][:, first:end], olds[t][:, first:end], keeps[t][:, first:end], MULT)
+
+        gate_rows(0, FIRST_PIECES)
+        products_by_vector(0, FIRST_PIECES)
+        gate_rows(1, 1)
 
         emb_turned = psum_held.tile([H, N], F32, name="emb_turned")
         for first, end in squares:
@@ -83,9 +95,12 @@ def tile_memory_s_kernel(tc, base, mem_old, emb, fw_emb, fw_mem, offs, out):
 
         old_turneds, gate_columns, keep_columns = {}, {}, {}
 
+        def round_block(t):
+            old_bf16s[t] = slots.tile([H, N], BF16, name="old_bf16")
+            nc.scalar.copy(old_bf16s[t][:], olds[t][:])
+
         def front(t):
-            old_bf16 = slots.tile([H, N], BF16, name="old_bf16")
-            nc.scalar.copy(old_bf16[:], olds[t][:])
+            old_bf16 = old_bf16s[t]
             old_turneds[t] = psum_turned.tile([H, N], F32, name="old_turned")
             for first, end in squares:
                 nc.tensor.transpose(old_turneds[t][:, first:end], olds[t][:, first:end], identity[:])
@@ -115,11 +130,16 @@ def tile_memory_s_kernel(tc, base, mem_old, emb, fw_emb, fw_mem, offs, out):
                     nc.tensor.transpose(bank[:, first:end], turned[:, first:end], identity[:])
                 nc.scalar.copy(product[:], bank[:])
 
-        front(1)
+        round_block(VECTOR_BLOCKS)
+        front(VECTOR_BLOCKS)
         place(0)
-        for t in range(1, T):
+        products_by_vector(1, 1)
+        place(1)
+        for t in range(VECTOR_BLOCKS, T):
             middle(t)
             if t + 1 < T:
-                front(t + 1)
+                round_block(t + 1)
             back(t)
+            if t + 1 < T:
+                front(t + 1)
             place(t)

@@ -9,7 +9,8 @@ SIGMOID, COPY = mybir.ActivationFunctionType.Sigmoid, mybir.ActivationFunctionTy
 
 FLOPS = 2 * H * N * (T + 1)
 
-FIRST_PIECES = 2
+LOAD_PIECES = 2
+FIRST_PIECES = 4
 
 VECTOR_BLOCKS = 2
 
@@ -41,7 +42,7 @@ def tile_memory_s_kernel(tc, base, mem_old, emb, fw_emb, fw_mem, offs, out):
         make_identity(nc, identity[:])
         for t in range(1, T):
             nc.gpsimd.dma_start(windows[t][:], base[t * H : (t + 1) * H, :])
-        for first, end in column_pieces(FIRST_PIECES):
+        for first, end in column_pieces(LOAD_PIECES):
             nc.sync.dma_start(emb_f32[:, first:end], emb[:, first:end])
             nc.sync.dma_start(olds[0][:, first:end], mem_old[0:H, first:end])
         nc.sync.dma_start(olds[1][:], mem_old[H : 2 * H, :])

@@ -37,19 +37,28 @@ def tile_memory_s_kernel(tc, base, mem_old, emb, fw_emb, fw_mem, offs, out):
         emb_f32 = held.tile([H, N], F32, name="emb_f32")
         olds = [slots.tile([H, N], F32, name="old") for t in range(T)]
         windows = [slots.tile([H, S], F32, name="window") for t in range(T)]
-        nc.gpsimd.dma_start(windows[0][:], base[0:H, :])
-        identity = held.tile([H, H], F32, name="identity")
-        make_identity(nc, identity[:])
-        for t in range(1, T):
-            nc.gpsimd.dma_start(windows[t][:], base[t * H : (t + 1) * H, :])
+        offsets = held.tile([H, N // 16], U16, name="offsets")
+
+        def load_old(t):
+            nc.sync.dma_start(olds[t][:], mem_old[t * H : (t + 1) * H, :])
+
+        def load_window(t):
+            nc.sync.dma_start(windows[t][:], base[t * H : (t + 1) * H, :])
+
         for first, end in column_pieces(LOAD_PIECES):
             nc.sync.dma_start(emb_f32[:, first:end], emb[:, first:end])
             nc.sync.dma_start(olds[0][:, first:end], mem_old[0:H, first:end])
-        nc.sync.dma_start(olds[1][:], mem_old[H : 2 * H, :])
-        offsets = held.tile([H, N // 16], U16, name="offsets")
+        load_window(0)
         nc.sync.dma_start(offsets[:], offs)
-        for t in range(2, T):
-            nc.sync.dma_start(olds[t][:], mem_old[t * H : (t + 1) * H, :])
+        load_old(1)
+        load_old(2)
+        load_window(1)
+        load_old(3)
+        load_window(2)
+        load_window(3)
+
+        identity = held.tile([H, H], F32, name="identity")
+        make_identity(nc, identity[:])
 
         spread_emb = held.tile([H, H], BF16, name="spread_emb")
         nc.vector.tensor_copy(spread_emb[:], column_emb[:].to_broadcast([H, H]))
@@ -68,12 +77,12 @@ def tile_memory_s_kernel(tc, base, mem_old, emb, fw_emb, fw_mem, offs, out):
 
         old_bf16s, gates, keeps = {}, {}, {}
 
-        def gate_rows(t, pieces):
+        def gate_rows(t, pieces, rounding_copy):
             old_bf16s[t] = slots.tile([H, N], BF16, name="old_bf16")
             gates[t] = slots.tile([H, N], F32, name="gate")
             keeps[t] = slots.tile([H, N], F32, name="keep")
             for first, end in column_pieces(pieces):
-                nc.vector.tensor_copy(old_bf16s[t][:, first:end], olds[t][:, first:end])
+                rounding_copy(old_bf16s[t][:, first:end], olds[t][:, first:end])
                 bank = psum_banks.tile([H, N], F32, name="bank")
                 logit = bank[:, 0 : end - first]
                 nc.tensor.matmul(logit, spread_emb[:], emb_bf16[:, first:end], start=True, stop=False)
@@ -86,9 +95,9 @@ def tile_memory_s_kernel(tc, base, mem_old, emb, fw_emb, fw_mem, offs, out):
                 nc.vector.tensor_tensor(writtens[t][:, first:end], emb_f32[:, first:end], gates[t][:, first:end], MULT)
                 nc.vector.tensor_tensor(kepts[t][:, first:end], olds[t][:, first:end], keeps[t][:, first:end], MULT)
 
-        gate_rows(0, FIRST_PIECES)
+        gate_rows(0, FIRST_PIECES, nc.vector.tensor_copy)
         products_by_vector(0, FIRST_PIECES)
-        gate_rows(1, 1)
+        gate_rows(1, 1, nc.scalar.copy)
 
         emb_turned = psum_held.tile([H, N], F32, name="emb_turned")
         for first, end in squares:

@@ -12,11 +12,11 @@ FLOPS = 2 * H * N * (T + 1)
 LOAD_PIECES = 2
 FIRST_PIECES = 4
 
-VECTOR_BLOCKS = 2
+VECTOR_COLUMNS = (N, N // 2, 0, 0)
 
 
-def column_pieces(pieces):
-    width = N // pieces
+def column_pieces(pieces, columns=N):
+    width = columns // pieces
     return [(piece * width, (piece + 1) * width) for piece in range(pieces)]
 
 
@@ -48,9 +48,12 @@ def tile_memory_s_kernel(tc, base, mem_old, emb, fw_emb, fw_mem, offs, out):
         for first, end in column_pieces(LOAD_PIECES):
             nc.sync.dma_start(emb_f32[:, first:end], emb[:, first:end])
             nc.sync.dma_start(olds[0][:, first:end], mem_old[0:H, first:end])
+        rest = slice(VECTOR_COLUMNS[1], N)
+        nc.sync.dma_start(olds[1][:, rest], mem_old[H : 2 * H, rest])
         load_window(0)
         nc.sync.dma_start(offsets[:], offs)
-        load_old(1)
+        mine = slice(0, VECTOR_COLUMNS[1])
+        nc.sync.dma_start(olds[1][:, mine], mem_old[H : 2 * H, mine])
         load_old(2)
         load_window(1)
         load_old(3)
@@ -75,13 +78,13 @@ def tile_memory_s_kernel(tc, base, mem_old, emb, fw_emb, fw_mem, offs, out):
             nc.vector.tensor_tensor(windows[t][:].indirect(offsets[:]), kepts[t][:], writtens[t][:], ADD)
             nc.sync.dma_start(out[t * H : (t + 1) * H, :], windows[t][:])
 
-        old_bf16s, gates, keeps = {}, {}, {}
+        old_bf16s = [slots.tile([H, N], BF16, name="old_bf16") for t in range(T)]
+        gates, keeps = {}, {}
 
         def gate_rows(t, pieces, rounding_copy):
-            old_bf16s[t] = slots.tile([H, N], BF16, name="old_bf16")
             gates[t] = slots.tile([H, N], F32, name="gate")
             keeps[t] = slots.tile([H, N], F32, name="keep")
-            for first, end in column_pieces(pieces):
+            for first, end in column_pieces(pieces, VECTOR_COLUMNS[t]):
                 rounding_copy(old_bf16s[t][:, first:end], olds[t][:, first:end])
                 bank = psum_banks.tile([H, N], F32, name="bank")
                 logit = bank[:, 0 : end - first]
@@ -91,65 +94,67 @@ def tile_memory_s_kernel(tc, base, mem_old, emb, fw_emb, fw_mem, offs, out):
                 nc.scalar.activation(keeps[t][:, first:end], logit, SIGMOID, scale=-1.0)
 
         def products_by_vector(t, pieces):
-            for first, end in column_pieces(pieces):
+            for first, end in column_pieces(pieces, VECTOR_COLUMNS[t]):
                 nc.vector.tensor_tensor(writtens[t][:, first:end], emb_f32[:, first:end], gates[t][:, first:end], MULT)
                 nc.vector.tensor_tensor(kepts[t][:, first:end], olds[t][:, first:end], keeps[t][:, first:end], MULT)
 
         gate_rows(0, FIRST_PIECES, nc.vector.tensor_copy)
         products_by_vector(0, FIRST_PIECES)
-        gate_rows(1, 1, nc.scalar.copy)
 
         emb_turned = psum_held.tile([H, N], F32, name="emb_turned")
         for first, end in squares:
             nc.tensor.transpose(emb_turned[:, first:end], emb_f32[:, first:end], identity[:])
 
+        def turned_squares(t):
+            return [(b, first, end) for b, (first, end) in enumerate(squares) if first >= VECTOR_COLUMNS[t]]
+
         old_turneds, gate_columns, keep_columns = {}, {}, {}
 
-        def round_block(t):
-            old_bf16s[t] = slots.tile([H, N], BF16, name="old_bf16")
-            nc.scalar.copy(old_bf16s[t][:], olds[t][:])
+        def round_rest(t):
+            nc.scalar.copy(old_bf16s[t][:, VECTOR_COLUMNS[t] : N], olds[t][:, VECTOR_COLUMNS[t] : N])
 
         def front(t):
-            old_bf16 = old_bf16s[t]
             old_turneds[t] = psum_turned.tile([H, N], F32, name="old_turned")
-            for first, end in squares:
+            for b, first, end in turned_squares(t):
                 nc.tensor.transpose(old_turneds[t][:, first:end], olds[t][:, first:end], identity[:])
             logit_columns = psum_held.tile([H, B], F32, name="logit_columns")
-            for b, (first, end) in enumerate(squares):
+            for b, first, end in turned_squares(t):
                 nc.tensor.matmul(logit_columns[:, b : b + 1], emb_bf16[:, first:end], spread_emb[:, 0:1], start=True, stop=False)
-                nc.tensor.matmul(logit_columns[:, b : b + 1], old_bf16[:, first:end], spread_mem[:, 0:1], start=False, stop=True)
+                nc.tensor.matmul(logit_columns[:, b : b + 1], old_bf16s[t][:, first:end], spread_mem[:, 0:1], start=False, stop=True)
+            made = slice(VECTOR_COLUMNS[t] // H, B)
             gate_columns[t] = slots.tile([H, B], F32, name="gate_column")
-            nc.scalar.activation(gate_columns[t][:], logit_columns[:], SIGMOID)
+            nc.scalar.activation(gate_columns[t][:, made], logit_columns[:, made], SIGMOID)
             keep_columns[t] = slots.tile([H, B], F32, name="keep_column")
-            nc.scalar.activation(keep_columns[t][:], logit_columns[:], SIGMOID, scale=-1.0)
+            nc.scalar.activation(keep_columns[t][:, made], logit_columns[:, made], SIGMOID, scale=-1.0)
 
         kept_turneds, written_turneds = {}, {}
 
         def middle(t):
             kept_turneds[t] = slots.tile([H, N], F32, name="kept_turned")
-            for b, (first, end) in enumerate(squares):
+            for b, first, end in turned_squares(t):
                 nc.scalar.activation(kept_turneds[t][:, first:end], old_turneds[t][:, first:end], COPY, scale=keep_columns[t][:, b : b + 1])
             written_turneds[t] = slots.tile([H, N], F32, name="written_turned")
-            for b, (first, end) in enumerate(squares):
+            for b, first, end in turned_squares(t):
                 nc.scalar.activation(written_turneds[t][:, first:end], emb_turned[:, first:end], COPY, scale=gate_columns[t][:, b : b + 1])
 
         def back(t):
             for turned, product in ((kept_turneds[t], kepts[t]), (written_turneds[t], writtens[t])):
                 bank = psum_banks.tile([H, N], F32, name="bank")
-                for first, end in squares:
+                for b, first, end in turned_squares(t):
                     nc.tensor.transpose(bank[:, first:end], turned[:, first:end], identity[:])
-                nc.scalar.copy(product[:], bank[:])
+                nc.scalar.copy(product[:, VECTOR_COLUMNS[t] : N], bank[:, VECTOR_COLUMNS[t] : N])
 
-        round_block(VECTOR_BLOCKS)
-        front(VECTOR_BLOCKS)
+        round_rest(1)
+        front(1)
+        gate_rows(1, 1, nc.scalar.copy)
         place(0)
-        products_by_vector(1, 1)
-        place(1)
-        for t in range(VECTOR_BLOCKS, T):
+        for t in range(1, T):
             middle(t)
             if t + 1 < T:
-                round_block(t + 1)
+                round_rest(t + 1)
             back(t)
             if t + 1 < T:
                 front(t + 1)
+            if VECTOR_COLUMNS[t] > 0:
+                products_by_vector(t, 1)
             place(t)

@@ -48,10 +48,10 @@ def tile_memory_s_kernel(tc, base, mem_old, emb, fw_emb, fw_mem, offs, out):
         for first, end in column_pieces(LOAD_PIECES):
             nc.sync.dma_start(emb_f32[:, first:end], emb[:, first:end])
             nc.sync.dma_start(olds[0][:, first:end], mem_old[0:H, first:end])
+        nc.sync.dma_start(offsets[:], offs)
         rest = slice(VECTOR_COLUMNS[1], N)
         nc.sync.dma_start(olds[1][:, rest], mem_old[H : 2 * H, rest])
         load_window(0)
-        nc.sync.dma_start(offsets[:], offs)
         mine = slice(0, VECTOR_COLUMNS[1])
         nc.sync.dma_start(olds[1][:, mine], mem_old[H : 2 * H, mine])
         load_old(2)
@@ -110,17 +110,17 @@ def tile_memory_s_kernel(tc, base, mem_old, emb, fw_emb, fw_mem, offs, out):
 
         old_turneds, gate_columns, keep_columns = {}, {}, {}
 
-        def round_rest(t):
-            nc.scalar.copy(old_bf16s[t][:, VECTOR_COLUMNS[t] : N], olds[t][:, VECTOR_COLUMNS[t] : N])
+        def round_rest(t, rounding_copy):
+            rounding_copy(old_bf16s[t][:, VECTOR_COLUMNS[t] : N], olds[t][:, VECTOR_COLUMNS[t] : N])
 
         def front(t):
-            old_turneds[t] = psum_turned.tile([H, N], F32, name="old_turned")
-            for b, first, end in turned_squares(t):
-                nc.tensor.transpose(old_turneds[t][:, first:end], olds[t][:, first:end], identity[:])
             logit_columns = psum_held.tile([H, B], F32, name="logit_columns")
             for b, first, end in turned_squares(t):
                 nc.tensor.matmul(logit_columns[:, b : b + 1], emb_bf16[:, first:end], spread_emb[:, 0:1], start=True, stop=False)
                 nc.tensor.matmul(logit_columns[:, b : b + 1], old_bf16s[t][:, first:end], spread_mem[:, 0:1], start=False, stop=True)
+            old_turneds[t] = psum_turned.tile([H, N], F32, name="old_turned")
+            for b, first, end in turned_squares(t):
+                nc.tensor.transpose(old_turneds[t][:, first:end], olds[t][:, first:end], identity[:])
             made = slice(VECTOR_COLUMNS[t] // H, B)
             gate_columns[t] = slots.tile([H, B], F32, name="gate_column")
             nc.scalar.activation(gate_columns[t][:, made], logit_columns[:, made], SIGMOID)
@@ -130,28 +130,29 @@ def tile_memory_s_kernel(tc, base, mem_old, emb, fw_emb, fw_mem, offs, out):
         kept_turneds, written_turneds = {}, {}
 
         def middle(t):
-            kept_turneds[t] = slots.tile([H, N], F32, name="kept_turned")
-            for b, first, end in turned_squares(t):
-                nc.scalar.activation(kept_turneds[t][:, first:end], old_turneds[t][:, first:end], COPY, scale=keep_columns[t][:, b : b + 1])
             written_turneds[t] = slots.tile([H, N], F32, name="written_turned")
             for b, first, end in turned_squares(t):
                 nc.scalar.activation(written_turneds[t][:, first:end], emb_turned[:, first:end], COPY, scale=gate_columns[t][:, b : b + 1])
+            kept_turneds[t] = slots.tile([H, N], F32, name="kept_turned")
+            for b, first, end in turned_squares(t):
+                nc.scalar.activation(kept_turneds[t][:, first:end], old_turneds[t][:, first:end], COPY, scale=keep_columns[t][:, b : b + 1])
 
         def back(t):
-            for turned, product in ((kept_turneds[t], kepts[t]), (written_turneds[t], writtens[t])):
+            for turned, product in ((written_turneds[t], writtens[t]), (kept_turneds[t], kepts[t])):
                 bank = psum_banks.tile([H, N], F32, name="bank")
                 for b, first, end in turned_squares(t):
                     nc.tensor.transpose(bank[:, first:end], turned[:, first:end], identity[:])
                 nc.scalar.copy(product[:, VECTOR_COLUMNS[t] : N], bank[:, VECTOR_COLUMNS[t] : N])
 
-        round_rest(1)
+        round_rest(1, nc.vector.tensor_copy)
         front(1)
-        gate_rows(1, 1, nc.scalar.copy)
         place(0)
         for t in range(1, T):
             middle(t)
+            if VECTOR_COLUMNS[t] > 0:
+                gate_rows(t, 1, nc.scalar.copy)
             if t + 1 < T:
-                round_rest(t + 1)
+                round_rest(t + 1, nc.scalar.copy)
             back(t)
             if t + 1 < T:
                 front(t + 1)

@@ -31,9 +31,7 @@ def tile_memory_s_kernel(tc, base, mem_old, emb, fw_emb, fw_mem, offs, out):
         tc.psum_pool(name="psum_banks", bufs=4) as psum_banks,
     ):
         column_emb = held.tile([H, 1], F32, name="column_emb")
-        nc.scalar.dma_start(column_emb[:], fw_emb)
         column_mem = held.tile([H, 1], F32, name="column_mem")
-        nc.scalar.dma_start(column_mem[:], fw_mem)
         emb_f32 = held.tile([H, N], F32, name="emb_f32")
         olds = [slots.tile([H, N], F32, name="old") for t in range(T)]
         windows = [slots.tile([H, S], F32, name="window") for t in range(T)]
@@ -45,13 +43,19 @@ def tile_memory_s_kernel(tc, base, mem_old, emb, fw_emb, fw_mem, offs, out):
         def load_window(t):
             nc.sync.dma_start(windows[t][:], base[t * H : (t + 1) * H, :])
 
-        for first, end in column_pieces(LOAD_PIECES):
+        def load_piece(first, end):
             nc.sync.dma_start(emb_f32[:, first:end], emb[:, first:end])
             nc.sync.dma_start(olds[0][:, first:end], mem_old[0:H, first:end])
-        nc.sync.dma_start(offsets[:], offs)
+
+        first_piece, last_piece = column_pieces(LOAD_PIECES)
+        load_piece(*first_piece)
+        nc.scalar.dma_start(column_emb[:], fw_emb)
+        nc.scalar.dma_start(column_mem[:], fw_mem)
+        load_piece(*last_piece)
         rest = slice(VECTOR_COLUMNS[1], N)
         nc.sync.dma_start(olds[1][:, rest], mem_old[H : 2 * H, rest])
         load_window(0)
+        nc.sync.dma_start(offsets[:], offs)
         mine = slice(0, VECTOR_COLUMNS[1])
         nc.sync.dma_start(olds[1][:, mine], mem_old[H : 2 * H, mine])
         load_old(2)

@@ -1,18 +1,16 @@
 import concourse.mybir as mybir
-from concourse.masks import make_identity
 
 H, T, S, N = 128, 4, 1024, 512
 B = N // H
+Q = 32
 F32, BF16, U16 = mybir.dt.float32, mybir.dt.bfloat16, mybir.dt.uint16
-ADD, MULT = mybir.AluOpType.add, mybir.AluOpType.mult
+ADD, MULT, IS_EQUAL = mybir.AluOpType.add, mybir.AluOpType.mult, mybir.AluOpType.is_equal
 SIGMOID, COPY = mybir.ActivationFunctionType.Sigmoid, mybir.ActivationFunctionType.Copy
 
 FLOPS = 2 * H * N * (T + 1)
 
 LOAD_PIECES = 2
 FIRST_PIECES = 4
-
-VECTOR_COLUMNS = (N, N // 2, 0, 0)
 
 
 def column_pieces(pieces, columns=N):
@@ -26,6 +24,7 @@ def tile_memory_s_kernel(tc, base, mem_old, emb, fw_emb, fw_mem, offs, out):
     with (
         tc.tile_pool(name="held", bufs=1) as held,
         tc.tile_pool(name="slots", bufs=T) as slots,
+        tc.tile_pool(name="turns", bufs=1) as turns,
         tc.psum_pool(name="psum_held", bufs=1) as psum_held,
         tc.psum_pool(name="psum_turned", bufs=2) as psum_turned,
         tc.psum_pool(name="psum_banks", bufs=4) as psum_banks,
@@ -52,20 +51,26 @@ def tile_memory_s_kernel(tc, base, mem_old, emb, fw_emb, fw_mem, offs, out):
         nc.scalar.dma_start(column_emb[:], fw_emb)
         nc.scalar.dma_start(column_mem[:], fw_mem)
         load_piece(*last_piece)
-        rest = slice(VECTOR_COLUMNS[1], N)
-        nc.sync.dma_start(olds[1][:, rest], mem_old[H : 2 * H, rest])
+        load_old(1)
         load_window(0)
         nc.sync.dma_start(offsets[:], offs)
-        mine = slice(0, VECTOR_COLUMNS[1])
-        nc.sync.dma_start(olds[1][:, mine], mem_old[H : 2 * H, mine])
         load_old(2)
         load_window(1)
         load_old(3)
         load_window(2)
         load_window(3)
 
+        ones = held.tile([H, Q], F32, name="ones")
+        nc.vector.memset(ones[:], 1.0)
+        count = held.tile([H, Q], F32, name="count", align_bytes=64)
+        nc.vector.tensor_tensor_scan(count[:], ones[:], ones[:], -1.0, op0=MULT, op1=ADD)
+        count_turned = held.tile([H, Q], F32, name="count_turned", align_bytes=64)
+        nc.vector.transpose(count_turned[:], count[:])
         identity = held.tile([H, H], F32, name="identity")
-        make_identity(nc, identity[:])
+        nc.vector.memset(identity[:], 0.0)
+        for block in range(0, H, Q):
+            own = slice(block, block + Q)
+            nc.vector.tensor_tensor(identity[own, own], count[own, :], count_turned[own, :], IS_EQUAL)
 
         spread_emb = held.tile([H, H], BF16, name="spread_emb")
         nc.vector.tensor_copy(spread_emb[:], column_emb[:].to_broadcast([H, H]))
@@ -75,6 +80,10 @@ def tile_memory_s_kernel(tc, base, mem_old, emb, fw_emb, fw_mem, offs, out):
         for first, end in column_pieces(FIRST_PIECES):
             nc.vector.tensor_copy(emb_bf16[:, first:end], emb_f32[:, first:end])
 
+        emb_turned = psum_held.tile([H, N], F32, name="emb_turned")
+        for first, end in squares:
+            nc.tensor.transpose(emb_turned[:, first:end], emb_f32[:, first:end], identity[:])
+
         kepts = [slots.tile([H, N], F32, name="kept") for t in range(T)]
         writtens = [slots.tile([H, N], F32, name="written") for t in range(T)]
 
@@ -82,84 +91,65 @@ def tile_memory_s_kernel(tc, base, mem_old, emb, fw_emb, fw_mem, offs, out):
             nc.vector.tensor_tensor(windows[t][:].indirect(offsets[:]), kepts[t][:], writtens[t][:], ADD)
             nc.sync.dma_start(out[t * H : (t + 1) * H, :], windows[t][:])
 
-        old_bf16s = [slots.tile([H, N], BF16, name="old_bf16") for t in range(T)]
-        gates, keeps = {}, {}
-
-        def gate_rows(t, pieces, rounding_copy):
-            gates[t] = slots.tile([H, N], F32, name="gate")
-            keeps[t] = slots.tile([H, N], F32, name="keep")
-            for first, end in column_pieces(pieces, VECTOR_COLUMNS[t]):
-                rounding_copy(old_bf16s[t][:, first:end], olds[t][:, first:end])
-                bank = psum_banks.tile([H, N], F32, name="bank")
-                logit = bank[:, 0 : end - first]
-                nc.tensor.matmul(logit, spread_emb[:], emb_bf16[:, first:end], start=True, stop=False)
-                nc.tensor.matmul(logit, spread_mem[:], old_bf16s[t][:, first:end], start=False, stop=True)
-                nc.scalar.activation(gates[t][:, first:end], logit, SIGMOID)
-                nc.scalar.activation(keeps[t][:, first:end], logit, SIGMOID, scale=-1.0)
-
-        def products_by_vector(t, pieces):
-            for first, end in column_pieces(pieces, VECTOR_COLUMNS[t]):
-                nc.vector.tensor_tensor(writtens[t][:, first:end], emb_f32[:, first:end], gates[t][:, first:end], MULT)
-                nc.vector.tensor_tensor(kepts[t][:, first:end], olds[t][:, first:end], keeps[t][:, first:end], MULT)
-
-        gate_rows(0, FIRST_PIECES, nc.vector.tensor_copy)
-        products_by_vector(0, FIRST_PIECES)
-
-        emb_turned = psum_held.tile([H, N], F32, name="emb_turned")
-        for first, end in squares:
-            nc.tensor.transpose(emb_turned[:, first:end], emb_f32[:, first:end], identity[:])
-
-        def turned_squares(t):
-            return [(b, first, end) for b, (first, end) in enumerate(squares) if first >= VECTOR_COLUMNS[t]]
+        old_bf16s, gate, keep = {}, held.tile([H, N], F32, name="gate"), held.tile([H, N], F32, name="keep")
+        old_bf16s[0] = slots.tile([H, N], BF16, name="old_bf16")
+        for first, end in column_pieces(FIRST_PIECES):
+            nc.vector.tensor_copy(old_bf16s[0][:, first:end], olds[0][:, first:end])
+            bank = psum_banks.tile([H, N], F32, name="bank")
+            logit = bank[:, 0 : end - first]
+            nc.tensor.matmul(logit, spread_emb[:], emb_bf16[:, first:end], start=True, stop=False)
+            nc.tensor.matmul(logit, spread_mem[:], old_bf16s[0][:, first:end], start=False, stop=True)
+            nc.scalar.activation(gate[:, first:end], logit, SIGMOID)
+            nc.scalar.activation(keep[:, first:end], logit, SIGMOID, scale=-1.0)
+        for first, end in column_pieces(FIRST_PIECES):
+            nc.vector.tensor_tensor(writtens[0][:, first:end], emb_f32[:, first:end], gate[:, first:end], MULT)
+            nc.vector.tensor_tensor(kepts[0][:, first:end], olds[0][:, first:end], keep[:, first:end], MULT)
 
         old_turneds, gate_columns, keep_columns = {}, {}, {}
 
-        def round_rest(t, rounding_copy):
-            rounding_copy(old_bf16s[t][:, VECTOR_COLUMNS[t] : N], olds[t][:, VECTOR_COLUMNS[t] : N])
+        def round_block(t, rounding_copy):
+            pool = slots if t < 2 else turns
+            old_bf16s[t] = pool.tile([H, N], BF16, name="old_bf16", tag="old_bf16" if t < 2 else "turn")
+            rounding_copy(old_bf16s[t][:], olds[t][:])
 
         def front(t):
             logit_columns = psum_held.tile([H, B], F32, name="logit_columns")
-            for b, first, end in turned_squares(t):
-                nc.tensor.matmul(logit_columns[:, b : b + 1], emb_bf16[:, first:end], spread_emb[:, 0:1], start=True, stop=False)
-                nc.tensor.matmul(logit_columns[:, b : b + 1], old_bf16s[t][:, first:end], spread_mem[:, 0:1], start=False, stop=True)
+            for b, (first, end) in enumerate(squares):
+                nc.tensor.matmul(logit_columns[:, b : b + 1], old_bf16s[t][:, first:end], spread_mem[:, 0:1], start=True, stop=False)
+                nc.tensor.matmul(logit_columns[:, b : b + 1], emb_bf16[:, first:end], spread_emb[:, 0:1], start=False, stop=True)
             old_turneds[t] = psum_turned.tile([H, N], F32, name="old_turned")
-            for b, first, end in turned_squares(t):
+            for first, end in squares:
                 nc.tensor.transpose(old_turneds[t][:, first:end], olds[t][:, first:end], identity[:])
-            made = slice(VECTOR_COLUMNS[t] // H, B)
             gate_columns[t] = slots.tile([H, B], F32, name="gate_column")
-            nc.scalar.activation(gate_columns[t][:, made], logit_columns[:, made], SIGMOID)
-            keep_columns[t] = slots.tile([H, B], F32, name="keep_column")
-            nc.scalar.activation(keep_columns[t][:, made], logit_columns[:, made], SIGMOID, scale=-1.0)
+            nc.scalar.activation(gate_columns[t][:], logit_columns[:], SIGMOID)
+            keep_columns[t] = turns.tile([H, B], F32, name="keep_column", tag="turn")
+            nc.scalar.activation(keep_columns[t][:], logit_columns[:], SIGMOID, scale=-1.0)
 
         kept_turneds, written_turneds = {}, {}
 
         def middle(t):
             written_turneds[t] = slots.tile([H, N], F32, name="written_turned")
-            for b, first, end in turned_squares(t):
+            for b, (first, end) in enumerate(squares):
                 nc.scalar.activation(written_turneds[t][:, first:end], emb_turned[:, first:end], COPY, scale=gate_columns[t][:, b : b + 1])
             kept_turneds[t] = slots.tile([H, N], F32, name="kept_turned")
-            for b, first, end in turned_squares(t):
+            for b, (first, end) in enumerate(squares):
                 nc.scalar.activation(kept_turneds[t][:, first:end], old_turneds[t][:, first:end], COPY, scale=keep_columns[t][:, b : b + 1])
 
         def back(t):
             for turned, product in ((written_turneds[t], writtens[t]), (kept_turneds[t], kepts[t])):
                 bank = psum_banks.tile([H, N], F32, name="bank")
-                for b, first, end in turned_squares(t):
+                for first, end in squares:
                     nc.tensor.transpose(bank[:, first:end], turned[:, first:end], identity[:])
-                nc.scalar.copy(product[:, VECTOR_COLUMNS[t] : N], bank[:, VECTOR_COLUMNS[t] : N])
+                nc.scalar.copy(product[:], bank[:])
 
-        round_rest(1, nc.vector.tensor_copy)
+        round_block(1, nc.vector.tensor_copy)
         front(1)
         place(0)
         for t in range(1, T):
             middle(t)
-            if VECTOR_COLUMNS[t] > 0:
-                gate_rows(t, 1, nc.scalar.copy)
             if t + 1 < T:
-                round_rest(t + 1, nc.scalar.copy)
+                round_block(t + 1, nc.scalar.copy)
             back(t)
             if t + 1 < T:
                 front(t + 1)
-            if VECTOR_COLUMNS[t] > 0:
-                products_by_vector(t, 1)
             place(t)

@@ -27,7 +27,7 @@ def tile_memory_s_kernel(tc, base, mem_old, emb, fw_emb, fw_mem, offs, out):
         tc.tile_pool(name="turns", bufs=1) as turns,
         tc.psum_pool(name="psum_held", bufs=1) as psum_held,
         tc.psum_pool(name="psum_turned", bufs=2) as psum_turned,
-        tc.psum_pool(name="psum_banks", bufs=4) as psum_banks,
+        tc.psum_pool(name="psum_banks", bufs=3) as psum_banks,
     ):
         column_emb = held.tile([H, 1], F32, name="column_emb")
         column_mem = held.tile([H, 1], F32, name="column_mem")
@@ -80,10 +80,6 @@ def tile_memory_s_kernel(tc, base, mem_old, emb, fw_emb, fw_mem, offs, out):
         for first, end in column_pieces(FIRST_PIECES):
             nc.vector.tensor_copy(emb_bf16[:, first:end], emb_f32[:, first:end])
 
-        emb_turned = psum_held.tile([H, N], F32, name="emb_turned")
-        for first, end in squares:
-            nc.tensor.transpose(emb_turned[:, first:end], emb_f32[:, first:end], identity[:])
-
         kepts = [slots.tile([H, N], F32, name="kept") for t in range(T)]
         writtens = [slots.tile([H, N], F32, name="written") for t in range(T)]
 
@@ -93,9 +89,14 @@ def tile_memory_s_kernel(tc, base, mem_old, emb, fw_emb, fw_mem, offs, out):
 
         old_bf16s, gate, keep = {}, held.tile([H, N], F32, name="gate"), held.tile([H, N], F32, name="keep")
         old_bf16s[0] = slots.tile([H, N], BF16, name="old_bf16")
-        for first, end in column_pieces(FIRST_PIECES):
+        first_banks = (
+            psum_banks.tile([H, N], F32, name="first_piece", tag="bank"),
+            psum_held.tile([H, N], F32, name="second_piece", tag="emb_turned_1"),
+            psum_turned.tile([H, N], F32, name="third_piece", tag="old_turned"),
+            psum_turned.tile([H, N], F32, name="fourth_piece", tag="old_turned"),
+        )
+        for (first, end), bank in zip(column_pieces(FIRST_PIECES), first_banks):
             nc.vector.tensor_copy(old_bf16s[0][:, first:end], olds[0][:, first:end])
-            bank = psum_banks.tile([H, N], F32, name="bank")
             logit = bank[:, 0 : end - first]
             nc.tensor.matmul(logit, spread_emb[:], emb_bf16[:, first:end], start=True, stop=False)
             nc.tensor.matmul(logit, spread_mem[:], old_bf16s[0][:, first:end], start=False, stop=True)
@@ -104,6 +105,14 @@ def tile_memory_s_kernel(tc, base, mem_old, emb, fw_emb, fw_mem, offs, out):
         for first, end in column_pieces(FIRST_PIECES):
             nc.vector.tensor_tensor(writtens[0][:, first:end], emb_f32[:, first:end], gate[:, first:end], MULT)
             nc.vector.tensor_tensor(kepts[0][:, first:end], olds[0][:, first:end], keep[:, first:end], MULT)
+
+        emb_turneds = []
+        for piece in range(LOAD_PIECES):
+            bank = psum_held.tile([H, N], F32, name=f"emb_turned_{piece}")
+            for b in range(piece * B // LOAD_PIECES, (piece + 1) * B // LOAD_PIECES):
+                first, end = squares[b]
+                emb_turneds.append(bank[:, first:end])
+                nc.tensor.transpose(emb_turneds[b], emb_f32[:, first:end], identity[:])
 
         old_turneds, gate_columns, keep_columns = {}, {}, {}
 
@@ -130,7 +139,7 @@ def tile_memory_s_kernel(tc, base, mem_old, emb, fw_emb, fw_mem, offs, out):
         def middle(t):
             written_turneds[t] = slots.tile([H, N], F32, name="written_turned")
             for b, (first, end) in enumerate(squares):
-                nc.scalar.activation(written_turneds[t][:, first:end], emb_turned[:, first:end], COPY, scale=gate_columns[t][:, b : b + 1])
+                nc.scalar.activation(written_turneds[t][:, first:end], emb_turneds[b], COPY, scale=gate_columns[t][:, b : b + 1])
             kept_turneds[t] = slots.tile([H, N], F32, name="kept_turned")
             for b, (first, end) in enumerate(squares):
                 nc.scalar.activation(kept_turneds[t][:, first:end], old_turneds[t][:, first:end], COPY, scale=keep_columns[t][:, b : b + 1])

@@ -29,8 +29,7 @@ def tile_memory_s_kernel(tc, base, mem_old, emb, fw_emb, fw_mem, offs, out):
         tc.psum_pool(name="psum_turned", bufs=2) as psum_turned,
         tc.psum_pool(name="psum_banks", bufs=3) as psum_banks,
     ):
-        column_emb = held.tile([H, 1], F32, name="column_emb")
-        column_mem = held.tile([H, 1], F32, name="column_mem")
+        weights_f32 = held.tile([H, 2, 8], F32, name="weights_f32")
         emb_f32 = held.tile([H, N], F32, name="emb_f32")
         olds = [slots.tile([H, N], F32, name="old") for t in range(T)]
         windows = [slots.tile([H, S], F32, name="window") for t in range(T)]
@@ -48,8 +47,8 @@ def tile_memory_s_kernel(tc, base, mem_old, emb, fw_emb, fw_mem, offs, out):
 
         first_piece, last_piece = column_pieces(LOAD_PIECES)
         load_piece(*first_piece)
-        nc.scalar.dma_start(column_emb[:], fw_emb)
-        nc.scalar.dma_start(column_mem[:], fw_mem)
+        nc.sync.dma_start(weights_f32[:, 0, 0:1], fw_emb)
+        nc.sync.dma_start(weights_f32[:, 1, 0:1], fw_mem)
         load_piece(*last_piece)
         load_old(1)
         load_window(0)
@@ -72,10 +71,10 @@ def tile_memory_s_kernel(tc, base, mem_old, emb, fw_emb, fw_mem, offs, out):
             own = slice(block, block + Q)
             nc.vector.tensor_tensor(identity[own, own], count[own, :], count_turned[own, :], IS_EQUAL)
 
-        spread_emb = held.tile([H, H], BF16, name="spread_emb")
-        nc.vector.tensor_copy(spread_emb[:], column_emb[:].to_broadcast([H, H]))
-        spread_mem = held.tile([H, H], BF16, name="spread_mem")
-        nc.vector.tensor_copy(spread_mem[:], column_mem[:].to_broadcast([H, H]))
+        weights = held.tile([H, 2], BF16, name="weights")
+        nc.vector.tensor_copy(weights[:], weights_f32[:, :, 0])
+        weight_emb, weight_mem = weights[:, 0:1], weights[:, 1:2]
+        spread_emb, spread_mem = weight_emb.to_broadcast([H, H]), weight_mem.to_broadcast([H, H])
         emb_bf16 = held.tile([H, N], BF16, name="emb_bf16")
         for first, end in column_pieces(FIRST_PIECES):
             nc.vector.tensor_copy(emb_bf16[:, first:end], emb_f32[:, first:end])
@@ -98,8 +97,8 @@ def tile_memory_s_kernel(tc, base, mem_old, emb, fw_emb, fw_mem, offs, out):
         for (first, end), bank in zip(column_pieces(FIRST_PIECES), first_banks):
             nc.vector.tensor_copy(old_bf16s[0][:, first:end], olds[0][:, first:end])
             logit = bank[:, 0 : end - first]
-            nc.tensor.matmul(logit, spread_emb[:], emb_bf16[:, first:end], start=True, stop=False)
-            nc.tensor.matmul(logit, spread_mem[:], old_bf16s[0][:, first:end], start=False, stop=True)
+            nc.tensor.matmul(logit, spread_emb, emb_bf16[:, first:end], start=True, stop=False)
+            nc.tensor.matmul(logit, spread_mem, old_bf16s[0][:, first:end], start=False, stop=True)
             nc.scalar.activation(gate[:, first:end], logit, SIGMOID)
             nc.scalar.activation(keep[:, first:end], logit, SIGMOID, scale=-1.0)
         for first, end in column_pieces(FIRST_PIECES):
@@ -124,8 +123,8 @@ def tile_memory_s_kernel(tc, base, mem_old, emb, fw_emb, fw_mem, offs, out):
         def front(t):
             logit_columns = psum_held.tile([H, B], F32, name="logit_columns")
             for b, (first, end) in enumerate(squares):
-                nc.tensor.matmul(logit_columns[:, b : b + 1], old_bf16s[t][:, first:end], spread_mem[:, 0:1], start=True, stop=False)
-                nc.tensor.matmul(logit_columns[:, b : b + 1], emb_bf16[:, first:end], spread_emb[:, 0:1], start=False, stop=True)
+                nc.tensor.matmul(logit_columns[:, b : b + 1], old_bf16s[t][:, first:end], weight_mem, start=True, stop=False)
+                nc.tensor.matmul(logit_columns[:, b : b + 1], emb_bf16[:, first:end], weight_emb, start=False, stop=True)
             old_turneds[t] = psum_turned.tile([H, N], F32, name="old_turned")
             for first, end in squares:
                 nc.tensor.transpose(old_turneds[t][:, first:end], olds[t][:, first:end], identity[:])

@@ -29,7 +29,8 @@ def tile_memory_s_kernel(tc, base, mem_old, emb, fw_emb, fw_mem, offs, out):
         tc.psum_pool(name="psum_turned", bufs=2) as psum_turned,
         tc.psum_pool(name="psum_banks", bufs=3) as psum_banks,
     ):
-        weights_f32 = held.tile([H, 2, 8], F32, name="weights_f32")
+        column_emb = held.tile([H, 1], F32, name="column_emb")
+        column_mem = held.tile([H, 1], F32, name="column_mem")
         emb_f32 = held.tile([H, N], F32, name="emb_f32")
         olds = [slots.tile([H, N], F32, name="old") for t in range(T)]
         windows = [slots.tile([H, S], F32, name="window") for t in range(T)]
@@ -47,8 +48,8 @@ def tile_memory_s_kernel(tc, base, mem_old, emb, fw_emb, fw_mem, offs, out):
 
         first_piece, last_piece = column_pieces(LOAD_PIECES)
         load_piece(*first_piece)
-        nc.sync.dma_start(weights_f32[:, 0, 0:1], fw_emb)
-        nc.sync.dma_start(weights_f32[:, 1, 0:1], fw_mem)
+        nc.scalar.dma_start(column_emb[:], fw_emb)
+        nc.scalar.dma_start(column_mem[:], fw_mem)
         load_piece(*last_piece)
         load_old(1)
         load_window(0)
@@ -71,10 +72,10 @@ def tile_memory_s_kernel(tc, base, mem_old, emb, fw_emb, fw_mem, offs, out):
             own = slice(block, block + Q)
             nc.vector.tensor_tensor(identity[own, own], count[own, :], count_turned[own, :], IS_EQUAL)
 
-        weights = held.tile([H, 2], BF16, name="weights")
-        nc.vector.tensor_copy(weights[:], weights_f32[:, :, 0])
-        weight_emb, weight_mem = weights[:, 0:1], weights[:, 1:2]
-        spread_emb, spread_mem = weight_emb.to_broadcast([H, H]), weight_mem.to_broadcast([H, H])
+        spread_emb = held.tile([H, H], BF16, name="spread_emb")
+        nc.vector.tensor_copy(spread_emb[:], column_emb[:].to_broadcast([H, H]))
+        spread_mem = held.tile([H, H], BF16, name="spread_mem")
+        nc.vector.tensor_copy(spread_mem[:], column_mem[:].to_broadcast([H, H]))
         emb_bf16 = held.tile([H, N], BF16, name="emb_bf16")
         for first, end in column_pieces(FIRST_PIECES):
             nc.vector.tensor_copy(emb_bf16[:, first:end], emb_f32[:, first:end])
@@ -97,8 +98,8 @@ def tile_memory_s_kernel(tc, base, mem_old, emb, fw_emb, fw_mem, offs, out):
         for (first, end), bank in zip(column_pieces(FIRST_PIECES), first_banks):
             nc.vector.tensor_copy(old_bf16s[0][:, first:end], olds[0][:, first:end])
             logit = bank[:, 0 : end - first]
-            nc.tensor.matmul(logit, spread_emb, emb_bf16[:, first:end], start=True, stop=False)
-            nc.tensor.matmul(logit, spread_mem, old_bf16s[0][:, first:end], start=False, stop=True)
+            nc.tensor.matmul(logit, spread_emb[:], emb_bf16[:, first:end], start=True, stop=False)
+            nc.tensor.matmul(logit, spread_mem[:], old_bf16s[0][:, first:end], start=False, stop=True)
             nc.scalar.activation(gate[:, first:end], logit, SIGMOID)
             nc.scalar.activation(keep[:, first:end], logit, SIGMOID, scale=-1.0)
         for first, end in column_pieces(FIRST_PIECES):
@@ -121,17 +122,23 @@ def tile_memory_s_kernel(tc, base, mem_old, emb, fw_emb, fw_mem, offs, out):
             rounding_copy(old_bf16s[t][:], olds[t][:])
 
         def front(t):
-            logit_columns = psum_held.tile([H, B], F32, name="logit_columns")
-            for b, (first, end) in enumerate(squares):
-                nc.tensor.matmul(logit_columns[:, b : b + 1], old_bf16s[t][:, first:end], weight_mem, start=True, stop=False)
-                nc.tensor.matmul(logit_columns[:, b : b + 1], emb_bf16[:, first:end], weight_emb, start=False, stop=True)
+            gate_columns[t] = slots.tile([H, B], F32, name="gate_column")
+            keep_columns[t] = turns.tile([H, B], F32, name="keep_column", tag="turn")
+            logit_banks = [psum_held.tile([H, B], F32, name="logit_columns")]
+            if t == 1:
+                logit_banks.append(psum_banks.tile([H, B], F32, name="logit_columns_of_half_1", tag="bank"))
+            share = B // len(logit_banks)
+            for half, logit_columns in enumerate(logit_banks):
+                made = slice(half * share, (half + 1) * share)
+                for b in range(half * share, (half + 1) * share):
+                    first, end = squares[b]
+                    nc.tensor.matmul(logit_columns[:, b : b + 1], old_bf16s[t][:, first:end], spread_mem[:, 0:1], start=True, stop=False)
+                    nc.tensor.matmul(logit_columns[:, b : b + 1], emb_bf16[:, first:end], spread_emb[:, 0:1], start=False, stop=True)
+                nc.scalar.activation(gate_columns[t][:, made], logit_columns[:, made], SIGMOID)
+                nc.scalar.activation(keep_columns[t][:, made], logit_columns[:, made], SIGMOID, scale=-1.0)
             old_turneds[t] = psum_turned.tile([H, N], F32, name="old_turned")
             for first, end in squares:
                 nc.tensor.transpose(old_turneds[t][:, first:end], olds[t][:, first:end], identity[:])
-            gate_columns[t] = slots.tile([H, B], F32, name="gate_column")
-            nc.scalar.activation(gate_columns[t][:], logit_columns[:], SIGMOID)
-            keep_columns[t] = turns.tile([H, B], F32, name="keep_column", tag="turn")
-            nc.scalar.activation(keep_columns[t][:], logit_columns[:], SIGMOID, scale=-1.0)
 
         kept_turneds, written_turneds = {}, {}
 

@@ -124,9 +124,10 @@ def tile_memory_s_kernel(tc, base, mem_old, emb, fw_emb, fw_mem, offs, out):
         def front(t):
             gate_columns[t] = slots.tile([H, B], F32, name="gate_column")
             keep_columns[t] = turns.tile([H, B], F32, name="keep_column", tag="turn")
-            logit_banks = [psum_held.tile([H, B], F32, name="logit_columns")]
-            if t == 1:
-                logit_banks.append(psum_banks.tile([H, B], F32, name="logit_columns_of_half_1", tag="bank"))
+            logit_banks = (
+                psum_held.tile([H, B], F32, name="logit_columns"),
+                psum_banks.tile([H, B], F32, name="logit_columns_of_half_1", tag="bank"),
+            )
             share = B // len(logit_banks)
             for half, logit_columns in enumerate(logit_banks):
                 made = slice(half * share, (half + 1) * share)

import concourse.mybir as mybir

H, T, S, N = 128, 4, 1024, 512
B = N // H
Q = 32
F32, BF16, U16 = mybir.dt.float32, mybir.dt.bfloat16, mybir.dt.uint16
ADD, MULT, IS_EQUAL = mybir.AluOpType.add, mybir.AluOpType.mult, mybir.AluOpType.is_equal
SIGMOID, COPY = mybir.ActivationFunctionType.Sigmoid, mybir.ActivationFunctionType.Copy

FLOPS = 2 * H * N * (T + 1)

LOAD_PIECES = 2
FIRST_PIECES = 4


def column_pieces(pieces, columns=N):
    width = columns // pieces
    return [(piece * width, (piece + 1) * width) for piece in range(pieces)]


def tile_memory_s_kernel(tc, base, mem_old, emb, fw_emb, fw_mem, offs, out):
    nc = tc.nc
    squares = column_pieces(B)
    with (
        tc.tile_pool(name="held", bufs=1) as held,
        tc.tile_pool(name="slots", bufs=T) as slots,
        tc.tile_pool(name="turns", bufs=1) as turns,
        tc.psum_pool(name="psum_held", bufs=1) as psum_held,
        tc.psum_pool(name="psum_turned", bufs=2) as psum_turned,
        tc.psum_pool(name="psum_banks", bufs=3) as psum_banks,
    ):
        column_emb = held.tile([H, 1], F32, name="column_emb")
        column_mem = held.tile([H, 1], F32, name="column_mem")
        emb_f32 = held.tile([H, N], F32, name="emb_f32")
        olds = [slots.tile([H, N], F32, name="old") for t in range(T)]
        windows = [slots.tile([H, S], F32, name="window") for t in range(T)]
        offsets = held.tile([H, N // 16], U16, name="offsets")

        def load_old(t):
            nc.sync.dma_start(olds[t][:], mem_old[t * H : (t + 1) * H, :])

        def load_window(t):
            nc.sync.dma_start(windows[t][:], base[t * H : (t + 1) * H, :])

        def load_piece(first, end):
            nc.sync.dma_start(emb_f32[:, first:end], emb[:, first:end])
            nc.sync.dma_start(olds[0][:, first:end], mem_old[0:H, first:end])

        first_piece, last_piece = column_pieces(LOAD_PIECES)
        load_piece(*first_piece)
        nc.scalar.dma_start(column_emb[:], fw_emb)
        nc.scalar.dma_start(column_mem[:], fw_mem)
        load_piece(*last_piece)
        load_old(1)
        load_window(0)
        nc.sync.dma_start(offsets[:], offs)
        load_old(2)
        load_window(1)
        load_old(3)
        load_window(2)
        load_window(3)

        ones = held.tile([H, Q], F32, name="ones")
        nc.vector.memset(ones[:], 1.0)
        count = held.tile([H, Q], F32, name="count", align_bytes=64)
        nc.vector.tensor_tensor_scan(count[:], ones[:], ones[:], -1.0, op0=MULT, op1=ADD)
        count_turned = held.tile([H, Q], F32, name="count_turned", align_bytes=64)
        nc.vector.transpose(count_turned[:], count[:])
        identity = held.tile([H, H], F32, name="identity")
        nc.vector.memset(identity[:], 0.0)
        for block in range(0, H, Q):
            own = slice(block, block + Q)
            nc.vector.tensor_tensor(identity[own, own], count[own, :], count_turned[own, :], IS_EQUAL)

        spread_emb = held.tile([H, H], BF16, name="spread_emb")
        nc.vector.tensor_copy(spread_emb[:], column_emb[:].to_broadcast([H, H]))
        spread_mem = held.tile([H, H], BF16, name="spread_mem")
        nc.vector.tensor_copy(spread_mem[:], column_mem[:].to_broadcast([H, H]))
        emb_bf16 = held.tile([H, N], BF16, name="emb_bf16")
        for first, end in column_pieces(FIRST_PIECES):
            nc.vector.tensor_copy(emb_bf16[:, first:end], emb_f32[:, first:end])

        kepts = [slots.tile([H, N], F32, name="kept") for t in range(T)]
        writtens = [slots.tile([H, N], F32, name="written") for t in range(T)]

        def place(t):
            nc.vector.tensor_tensor(windows[t][:].indirect(offsets[:]), kepts[t][:], writtens[t][:], ADD)
            nc.sync.dma_start(out[t * H : (t + 1) * H, :], windows[t][:])

        old_bf16s, gate, keep = {}, held.tile([H, N], F32, name="gate"), held.tile([H, N], F32, name="keep")
        old_bf16s[0] = slots.tile([H, N], BF16, name="old_bf16")
        first_banks = (
            psum_banks.tile([H, N], F32, name="first_piece", tag="bank"),
            psum_held.tile([H, N], F32, name="second_piece", tag="emb_turned_1"),
            psum_turned.tile([H, N], F32, name="third_piece", tag="old_turned"),
            psum_turned.tile([H, N], F32, name="fourth_piece", tag="old_turned"),
        )
        for (first, end), bank in zip(column_pieces(FIRST_PIECES), first_banks):
            nc.vector.tensor_copy(old_bf16s[0][:, first:end], olds[0][:, first:end])
            logit = bank[:, 0 : end - first]
            nc.tensor.matmul(logit, spread_emb[:], emb_bf16[:, first:end], start=True, stop=False)
            nc.tensor.matmul(logit, spread_mem[:], old_bf16s[0][:, first:end], start=False, stop=True)
            nc.scalar.activation(gate[:, first:end], logit, SIGMOID)
            nc.scalar.activation(keep[:, first:end], logit, SIGMOID, scale=-1.0)
        for first, end in column_pieces(FIRST_PIECES):
            nc.vector.tensor_tensor(writtens[0][:, first:end], emb_f32[:, first:end], gate[:, first:end], MULT)
            nc.vector.tensor_tensor(kepts[0][:, first:end], olds[0][:, first:end], keep[:, first:end], MULT)

        emb_turneds = []
        for piece in range(LOAD_PIECES):
            bank = psum_held.tile([H, N], F32, name=f"emb_turned_{piece}")
            for b in range(piece * B // LOAD_PIECES, (piece + 1) * B // LOAD_PIECES):
                first, end = squares[b]
                emb_turneds.append(bank[:, first:end])
                nc.tensor.transpose(emb_turneds[b], emb_f32[:, first:end], identity[:])

        old_turneds, gate_columns, keep_columns = {}, {}, {}

        def round_block(t, rounding_copy):
            pool = slots if t < 2 else turns
            old_bf16s[t] = pool.tile([H, N], BF16, name="old_bf16", tag="old_bf16" if t < 2 else "turn")
            rounding_copy(old_bf16s[t][:], olds[t][:])

        def front(t):
            gate_columns[t] = slots.tile([H, B], F32, name="gate_column")
            keep_columns[t] = turns.tile([H, B], F32, name="keep_column", tag="turn")
            logit_banks = (
                psum_held.tile([H, B], F32, name="logit_columns"),
                psum_banks.tile([H, B], F32, name="logit_columns_of_half_1", tag="bank"),
            )
            share = B // len(logit_banks)
            for half, logit_columns in enumerate(logit_banks):
                made = slice(half * share, (half + 1) * share)
                for b in range(half * share, (half + 1) * share):
                    first, end = squares[b]
                    nc.tensor.matmul(logit_columns[:, b : b + 1], old_bf16s[t][:, first:end], spread_mem[:, 0:1], start=True, stop=False)
                    nc.tensor.matmul(logit_columns[:, b : b + 1], emb_bf16[:, first:end], spread_emb[:, 0:1], start=False, stop=True)
                nc.scalar.activation(gate_columns[t][:, made], logit_columns[:, made], SIGMOID)
                nc.scalar.activation(keep_columns[t][:, made], logit_columns[:, made], SIGMOID, scale=-1.0)
            old_turneds[t] = psum_turned.tile([H, N], F32, name="old_turned")
            for first, end in squares:
                nc.tensor.transpose(old_turneds[t][:, first:end], olds[t][:, first:end], identity[:])

        kept_turneds, written_turneds = {}, {}

        def middle(t):
            written_turneds[t] = slots.tile([H, N], F32, name="written_turned")
            for b, (first, end) in enumerate(squares):
                nc.scalar.activation(written_turneds[t][:, first:end], emb_turneds[b], COPY, scale=gate_columns[t][:, b : b + 1])
            kept_turneds[t] = slots.tile([H, N], F32, name="kept_turned")
            for b, (first, end) in enumerate(squares):
                nc.scalar.activation(kept_turneds[t][:, first:end], old_turneds[t][:, first:end], COPY, scale=keep_columns[t][:, b : b + 1])

        def back(t):
            for turned, product in ((written_turneds[t], writtens[t]), (kept_turneds[t], kepts[t])):
                bank = psum_banks.tile([H, N], F32, name="bank")
                for first, end in squares:
                    nc.tensor.transpose(bank[:, first:end], turned[:, first:end], identity[:])
                nc.scalar.copy(product[:], bank[:])

        round_block(1, nc.vector.tensor_copy)
        front(1)
        place(0)
        for t in range(1, T):
            middle(t)
            if t + 1 < T:
                round_block(t + 1, nc.scalar.copy)
            back(t)
            if t + 1 < T:
                front(t + 1)
            place(t)
